import numpy as np
import ml_dtypes


def mxq(x, axis, fmt="e4m3"):
    dtype, down = {"e4m3": (ml_dtypes.float8_e4m3fn, 7), "e5m2": (ml_dtypes.float8_e5m2, 14)}[fmt]
    v = np.moveaxis(np.asarray(x, np.float32).astype(ml_dtypes.bfloat16).astype(np.float64), axis, -1)
    blocks = v.reshape(v.shape[:-1] + (-1, 32))
    amax = np.abs(blocks).max(-1, keepdims=True)
    byte = np.maximum(np.where(amax > 0, np.frexp(amax)[1] - 1 + 127, 0) - down, 1)
    scale = np.exp2(byte - 127.0)
    codes = (blocks / scale).astype(np.float32).astype(dtype).astype(np.float64)
    return np.moveaxis((codes * scale).reshape(v.shape), -1, axis)


WIDE = False


def mx_kscale(k):
    if not WIDE:
        return np.ones(k)
    levels = np.array([10, -10, 5, -5, 0])
    a = np.random.permutation(np.resize(levels, k // 512 * 4)).reshape(k // 512, 4)
    idx = np.arange(k)
    return np.exp2(a[idx // 512, idx % 128 // 32])


BF16 = ml_dtypes.bfloat16


def bf(x):
    return np.asarray(x, np.float32).astype(BF16)


def f64(x):
    return np.asarray(x).astype(np.float64)


E2M1 = np.array([0.0, 0.5, 1.0, 1.5, 2.0, 3.0, 4.0, 6.0, -0.0, -0.5, -1.0, -1.5, -2.0, -3.0, -4.0, -6.0])


def pack_weight(w, fmt):
    k, n = w.shape
    w = f64(bf(w)).reshape(k // 32, 32, n)
    amax = np.abs(w).max(1)
    if fmt == "e4m3":
        byte = np.frexp(amax)[1] - 1 + 127 - 7
    else:
        mant, ex = np.frexp(amax / 6.0)
        byte = np.where(mant > 0.5, ex, ex - 1) + 127
    byte = np.clip(np.where(amax > 0, byte, 1), 1, 254)
    scaled = (w * np.exp2(127.0 - byte)[:, None, :]).reshape(k, n).astype(np.float32)
    by_word = np.ascontiguousarray(scaled.reshape(k // 512, 128, 4, n).transpose(0, 1, 3, 2))
    if fmt == "e4m3":
        words = by_word.astype(ml_dtypes.float8_e4m3fn).view(np.uint8)
    else:
        c = by_word.astype(ml_dtypes.float4_e2m1fn).view(np.uint8) & 0xF
        words = c[..., 0::2] | (c[..., 1::2] << 4)
    return np.ascontiguousarray(words), np.ascontiguousarray(byte.astype(np.uint8).reshape(k // 512, 16, n))


def unpack_weight(words, scales, fmt):
    g, p, n, _ = words.shape
    if fmt == "e4m3":
        vals = np.ascontiguousarray(words).view(ml_dtypes.float8_e4m3fn).astype(np.float64)
    else:
        nib = np.empty((g, p, n, 4), np.uint8)
        nib[..., 0::2] = words & 0xF
        nib[..., 1::2] = words >> 4
        vals = E2M1[nib]
    vals = vals * np.repeat(np.exp2(scales.astype(np.float64) - 127.0), 8, axis=1)[..., None]
    return vals.transpose(0, 1, 3, 2).reshape(g * 512, n)

def pack4(w):
    words, scales = pack_weight(w, "e2m1")
    return words.reshape(words.shape[0], 128, -1), scales


def unpack4(words, scales):
    return unpack_weight(words.reshape(words.shape[0], 128, -1, 2), scales, "e2m1")


B, IMG, P0, P1, C, F = 2, 512, 8, 16, 2, 512
E0, E1 = IMG // P0, IMG // P1
N0, N1 = E0 * E0, E1 * E1
D0, D1 = P0 * P0 * C, P1 * P1 * C


def setup_inputs():
    s = mx_kscale(D1)
    flat = np.random.standard_normal((B, N1, D1)) * s
    img = flat.reshape(B, E1, E1, P1, P1, C).transpose(0, 1, 3, 2, 4, 5).reshape(B, IMG, IMG, C)
    encoded = img.reshape(B, E0, P0, E0, P0, C).transpose(0, 1, 3, 2, 4, 5).reshape(B, N0, D0)
    words, scales = pack4(np.random.standard_normal((D1, F)) / np.sqrt(D1) / s[:, None])
    return {"encoded": bf(encoded),
            "W_words": words,
            "W_scales": scales,
            "b": bf(np.random.standard_normal(F) * 0.3),
            "pos_emb": bf(np.random.standard_normal((N1, F)) * 0.5)}


def reference(encoded, W_words, W_scales, b, pos_emb):
    x = f64(encoded).reshape(-1, E0, E0, P0, P0, C)
    img = x.transpose(0, 1, 3, 2, 4, 5).reshape(-1, IMG, IMG, C)
    new_patches = img.reshape(-1, E1, P1, E1, P1, C).transpose(0, 1, 3, 2, 4, 5)
    flat = new_patches.reshape(-1, N1, D1)
    return (mxq(flat, 2, "e4m3") @ unpack4(W_words, W_scales)) + f64(b) + f64(pos_emb)

@@ -1,0 +1,160 @@
+from contextlib import ExitStack
+
+import concourse.mybir as mybir
+from concourse.masks import make_identity
+
+F32 = mybir.dt.float32
+BF16 = mybir.dt.bfloat16
+I32 = mybir.dt.int32
+U32 = mybir.dt.uint32
+U8 = mybir.dt.uint8
+FP8X4 = mybir.dt.float8_e4m3fn_x4
+FP4X4 = mybir.dt.float4_e2m1fn_x4
+ADD = mybir.AluOpType.add
+
+P = 128
+IMAGES = 2
+TOKENS = 1024
+K = 512
+FEATURES = 512
+TOKENS_PER_PARTITION = TOKENS // P
+GROUP_TILES = 4
+TAU_HALVES = TOKENS_PER_PARTITION // GROUP_TILES
+GROUPS = TAU_HALVES * IMAGES
+TILES = GROUPS * GROUP_TILES
+BANK_TILES = 2
+WORDS = K // 2
+HALF_WORDS = WORDS // 2
+
+FLOPS = 2 * IMAGES * TOKENS * K * FEATURES
+
+
+def tile_resampling_kernel(tc, encoded, W_words, W_scales, b, pos_emb, out):
+    nc = tc.nc
+    with ExitStack() as ctx:
+        keep = ctx.enter_context(tc.tile_pool(name="keep", bufs=1))
+        xt_pool = ctx.enter_context(tc.psum_pool(name="xt_pool", bufs=4))
+        acc_pool = ctx.enter_context(tc.psum_pool(name="acc_pool", bufs=4))
+
+        x_sb = keep.tile([P, GROUPS, 2, GROUP_TILES * K // 2], BF16)
+        sorted_words = keep.tile([P, TILES, WORDS], F32)
+        grouped = keep.tile([P, TILES // BANK_TILES, BANK_TILES * P * 4], BF16, align_bytes=64)
+        x_codes = keep.tile([P, TILES * P], U32, align_bytes=64)
+        x_scales = keep.tile([P, TILES * P], U8, align_bytes=64)
+        w_codes = keep.tile([P, 2 * FEATURES], U8, align_bytes=64)
+        w_scales = keep.tile([P, FEATURES], U8, align_bytes=64)
+        pos_sb = keep.tile([P, TOKENS_PER_PARTITION, FEATURES], BF16)
+        pos_b = keep.tile([P, TOKENS_PER_PARTITION, FEATURES], F32)
+        out_sb = keep.tile([P, IMAGES, TOKENS_PER_PARTITION, FEATURES], F32)
+        ident = keep.tile([P, P], F32)
+        ones = keep.tile([P, P], BF16)
+        b_row = keep.tile([P, FEATURES], BF16)
+        b_all = keep.tile([P, FEATURES], F32)
+
+        enc_view = encoded.rearrange(
+            "i (y s a h e) d -> i s h y a (e d)", y=32, s=2, a=4, h=TAU_HALVES, e=2 * GROUP_TILES
+        )
+        pos_view = pos_emb.rearrange("(p t) f -> p t f", t=TOKENS_PER_PARTITION)
+        out_view = out.rearrange("i (p t) f -> i p t f", t=TOKENS_PER_PARTITION)
+
+        def load_group(g):
+            h, i = divmod(g, IMAGES)
+            for s in range(2):
+                nc.sync.dma_start(out=x_sb[:, g, s, :], in_=enc_view[i, s, h])
+
+        def load_pos(h):
+            taus = slice(h * GROUP_TILES, (h + 1) * GROUP_TILES)
+            nc.sync.dma_start(out=pos_sb[:, taus, :], in_=pos_view[:, taus, :])
+
+        def add_bias_to_pos(h):
+            for tau in range(h * GROUP_TILES, (h + 1) * GROUP_TILES):
+                nc.gpsimd.tensor_tensor(out=pos_b[:, tau, :], in0=pos_sb[:, tau, :], in1=b_all[:], op=ADD)
+
+        def sort_group(g):
+            for tl in range(GROUP_TILES):
+                for s in range(2):
+                    src = x_sb[:, g, s, tl * WORDS : (tl + 1) * WORDS].bitcast(F32)
+                    dst = sorted_words[:, g * GROUP_TILES + tl, s * HALF_WORDS : (s + 1) * HALF_WORDS]
+                    nc.scalar.copy(
+                        out=dst.rearrange("p (r c w) -> p r c w", r=8, c=2),
+                        in_=src.rearrange("p (c r w) -> p r c w", c=2, r=8),
+                    )
+
+        def transpose_group(g):
+            banks = []
+            for half in range(GROUP_TILES // BANK_TILES):
+                xt = xt_pool.tile([P, BANK_TILES, 2, P], F32)
+                for l in range(BANK_TILES):
+                    tile_index = g * GROUP_TILES + half * BANK_TILES + l
+                    planes = sorted_words[:, tile_index, :].rearrange("p (j u) -> p u j", u=2)
+                    for u in range(2):
+                        nc.tensor.transpose(xt[:, l, u, :], planes[:, u, :], ident[:])
+                banks.append(xt)
+            return banks
+
+        def quantise_group(g, banks):
+            for half in range(GROUP_TILES // BANK_TILES):
+                bank = g * (GROUP_TILES // BANK_TILES) + half
+                cols = slice(bank * BANK_TILES * P, (bank + 1) * BANK_TILES * P)
+                nc.scalar.copy(
+                    out=grouped[:, bank, :].bitcast(F32).rearrange("p (l m u) -> p l m u", l=BANK_TILES, u=2),
+                    in_=banks[half][:].rearrange("p l u m -> p l m u"),
+                )
+                nc.vector.quantize_mx(
+                    out=x_codes[:, cols].bitcast(FP8X4), scales=x_scales[:, cols], in_=grouped[:, bank, :]
+                )
+
+        def project_group(g):
+            h, i = divmod(g, IMAGES)
+            for tl in range(GROUP_TILES):
+                tau = h * GROUP_TILES + tl
+                cols = slice((g * GROUP_TILES + tl) * P, (g * GROUP_TILES + tl + 1) * P)
+                acc = acc_pool.tile([P, FEATURES], F32, tag="acc")
+                nc.tensor.matmul_mx(
+                    out=acc[:],
+                    lhsT=x_codes[:, cols].bitcast(FP8X4),
+                    lhsT_scale=x_scales[:, cols],
+                    rhs=w_codes[:].bitcast(FP4X4),
+                    rhs_scale=w_scales[:],
+                    start=True,
+                    stop=True,
+                )
+                nc.vector.tensor_tensor(out=out_sb[:, i, tau, :], in0=acc[:], in1=pos_b[:, tau, :], op=ADD)
+                if tl % 2 == 1:
+                    taus = slice(tau - 1, tau + 1)
+                    nc.sync.dma_start(out=out_view[i][:, taus, :], in_=out_sb[:, i, taus, :])
+
+        nc.vector.memset(w_scales[:].bitcast(I32), 0)
+        nc.vector.memset(b_row[:], 0.0)
+        nc.vector.memset(ones[:], 1.0)
+        make_identity(nc, ident[:])
+
+        nc.scalar.dma_start(out=b_row[0:1, :], in_=b.rearrange("(o f) -> o f", o=1))
+        load_group(0)
+        nc.sync.dma_start(out=w_codes[:].bitcast(I32), in_=W_words[0].bitcast(I32))
+        for quadrant in range(4):
+            nc.sync.dma_start(
+                out=w_scales[32 * quadrant : 32 * quadrant + 4, :].bitcast(I32),
+                in_=W_scales[0, 4 * quadrant : 4 * quadrant + 4, :].bitcast(I32),
+            )
+        load_pos(0)
+        load_group(1)
+        load_group(2)
+        load_pos(1)
+        load_group(3)
+
+        b_psum = acc_pool.tile([P, FEATURES], F32, tag="acc")
+        nc.tensor.matmul(out=b_psum[:], lhsT=ones[:], rhs=b_row[:], start=True, stop=True)
+        nc.scalar.copy(out=b_all[:], in_=b_psum[:])
+        add_bias_to_pos(0)
+        add_bias_to_pos(1)
+
+        sort_group(0)
+        banks = transpose_group(0)
+        for g in range(GROUPS):
+            if g + 1 < GROUPS:
+                sort_group(g + 1)
+            quantise_group(g, banks)
+            if g + 1 < GROUPS:
+                banks = transpose_group(g + 1)
+            project_group(g)

@@ -18,11 +18,11 @@ TOKENS = 1024
 K = 512
 FEATURES = 512
 TOKENS_PER_PARTITION = TOKENS // P
-GROUP_TILES = 4
-TAU_HALVES = TOKENS_PER_PARTITION // GROUP_TILES
-GROUPS = TAU_HALVES * IMAGES
-TILES = GROUPS * GROUP_TILES
-BANK_TILES = 2
+LOAD_TILES = 4
+TAU_HALVES = TOKENS_PER_PARTITION // LOAD_TILES
+TILES = IMAGES * TOKENS_PER_PARTITION
+STEP_TILES = 2
+STEPS = TILES // STEP_TILES
 WORDS = K // 2
 HALF_WORDS = WORDS // 2
 
@@ -35,12 +35,13 @@ def tile_resampling_kernel(tc, encoded, W_words, W_scales, b, pos_emb, out):
         keep = ctx.enter_context(tc.tile_pool(name="keep", bufs=1))
         xt_pool = ctx.enter_context(tc.psum_pool(name="xt_pool", bufs=4))
         acc_pool = ctx.enter_context(tc.psum_pool(name="acc_pool", bufs=4))
+        ctx.enter_context(tc.manual_schedule())
 
-        x_sb = keep.tile([P, GROUPS, 2, GROUP_TILES * K // 2], BF16)
-        sorted_words = keep.tile([P, TILES, WORDS], F32)
-        grouped = keep.tile([P, TILES // BANK_TILES, BANK_TILES * P * 4], BF16, align_bytes=64)
-        x_codes = keep.tile([P, TILES * P], U32, align_bytes=64)
-        x_scales = keep.tile([P, TILES * P], U8, align_bytes=64)
+        x_sb = keep.tile([P, IMAGES, TAU_HALVES, 2, LOAD_TILES * K // 2], BF16)
+        sorted_words = keep.tile([P, STEPS, STEP_TILES, WORDS], F32)
+        grouped = keep.tile([P, STEPS, STEP_TILES * P * 4], BF16, align_bytes=64)
+        x_codes = keep.tile([P, STEPS, STEP_TILES * P], U32, align_bytes=64)
+        x_scales = keep.tile([P, STEPS, STEP_TILES * P], U8, align_bytes=64)
         w_codes = keep.tile([P, 2 * FEATURES], U8, align_bytes=64)
         w_scales = keep.tile([P, FEATURES], U8, align_bytes=64)
         pos_sb = keep.tile([P, TOKENS_PER_PARTITION, FEATURES], BF16)
@@ -52,77 +53,69 @@ def tile_resampling_kernel(tc, encoded, W_words, W_scales, b, pos_emb, out):
         b_all = keep.tile([P, FEATURES], F32)
 
         enc_view = encoded.rearrange(
-            "i (y s a h e) d -> i s h y a (e d)", y=32, s=2, a=4, h=TAU_HALVES, e=2 * GROUP_TILES
+            "i (y s a h e) d -> i s h y a (e d)", y=32, s=2, a=4, h=TAU_HALVES, e=2 * LOAD_TILES
         )
         pos_view = pos_emb.rearrange("(p t) f -> p t f", t=TOKENS_PER_PARTITION)
         out_view = out.rearrange("i (p t) f -> i p t f", t=TOKENS_PER_PARTITION)
 
-        def load_group(g):
-            h, i = divmod(g, IMAGES)
+        def load_tokens(i, h):
             for s in range(2):
-                nc.sync.dma_start(out=x_sb[:, g, s, :], in_=enc_view[i, s, h])
+                nc.sync.dma_start(out=x_sb[:, i, h, s, :], in_=enc_view[i, s, h])
 
-        def load_pos(h):
-            taus = slice(h * GROUP_TILES, (h + 1) * GROUP_TILES)
+        def load_pos(pair):
+            taus = slice(pair * STEP_TILES, (pair + 1) * STEP_TILES)
             nc.sync.dma_start(out=pos_sb[:, taus, :], in_=pos_view[:, taus, :])
 
-        def add_bias_to_pos(h):
-            for tau in range(h * GROUP_TILES, (h + 1) * GROUP_TILES):
-                nc.gpsimd.tensor_tensor(out=pos_b[:, tau, :], in0=pos_sb[:, tau, :], in1=b_all[:], op=ADD)
-
-        def sort_group(g):
-            for tl in range(GROUP_TILES):
+        def sort_step(n):
+            pair, i = divmod(n, IMAGES)
+            for l in range(STEP_TILES):
+                h, tl = divmod(pair * STEP_TILES + l, LOAD_TILES)
                 for s in range(2):
-                    src = x_sb[:, g, s, tl * WORDS : (tl + 1) * WORDS].bitcast(F32)
-                    dst = sorted_words[:, g * GROUP_TILES + tl, s * HALF_WORDS : (s + 1) * HALF_WORDS]
+                    src = x_sb[:, i, h, s, tl * WORDS : (tl + 1) * WORDS].bitcast(F32)
+                    dst = sorted_words[:, n, l, s * HALF_WORDS : (s + 1) * HALF_WORDS]
                     nc.scalar.copy(
                         out=dst.rearrange("p (r c w) -> p r c w", r=8, c=2),
                         in_=src.rearrange("p (c r w) -> p r c w", c=2, r=8),
                     )
 
-        def transpose_group(g):
-            banks = []
-            for half in range(GROUP_TILES // BANK_TILES):
-                xt = xt_pool.tile([P, BANK_TILES, 2, P], F32)
-                for l in range(BANK_TILES):
-                    tile_index = g * GROUP_TILES + half * BANK_TILES + l
-                    planes = sorted_words[:, tile_index, :].rearrange("p (j u) -> p u j", u=2)
-                    for u in range(2):
-                        nc.tensor.transpose(xt[:, l, u, :], planes[:, u, :], ident[:])
-                banks.append(xt)
-            return banks
+        def transpose_step(n):
+            xt = xt_pool.tile([P, STEP_TILES, 2, P], F32)
+            for l in range(STEP_TILES):
+                planes = sorted_words[:, n, l, :].rearrange("p (j u) -> p u j", u=2)
+                for u in range(2):
+                    nc.tensor.transpose(xt[:, l, u, :], planes[:, u, :], ident[:])
+            return xt
 
-        def quantise_group(g, banks):
-            for half in range(GROUP_TILES // BANK_TILES):
-                bank = g * (GROUP_TILES // BANK_TILES) + half
-                cols = slice(bank * BANK_TILES * P, (bank + 1) * BANK_TILES * P)
-                nc.scalar.copy(
-                    out=grouped[:, bank, :].bitcast(F32).rearrange("p (l m u) -> p l m u", l=BANK_TILES, u=2),
-                    in_=banks[half][:].rearrange("p l u m -> p l m u"),
-                )
-                nc.vector.quantize_mx(
-                    out=x_codes[:, cols].bitcast(FP8X4), scales=x_scales[:, cols], in_=grouped[:, bank, :]
-                )
+        def quantise_step(n, xt):
+            nc.scalar.copy(
+                out=grouped[:, n, :].bitcast(F32).rearrange("p (l m u) -> p l m u", l=STEP_TILES, u=2),
+                in_=xt[:].rearrange("p l u m -> p l m u"),
+            )
+            nc.vector.quantize_mx(out=x_codes[:, n, :].bitcast(FP8X4), scales=x_scales[:, n, :], in_=grouped[:, n, :])
 
-        def project_group(g):
-            h, i = divmod(g, IMAGES)
-            for tl in range(GROUP_TILES):
-                tau = h * GROUP_TILES + tl
-                cols = slice((g * GROUP_TILES + tl) * P, (g * GROUP_TILES + tl + 1) * P)
+        def multiply_step(n):
+            sums = []
+            for l in range(STEP_TILES):
+                cols = slice(l * P, (l + 1) * P)
                 acc = acc_pool.tile([P, FEATURES], F32, tag="acc")
                 nc.tensor.matmul_mx(
                     out=acc[:],
-                    lhsT=x_codes[:, cols].bitcast(FP8X4),
-                    lhsT_scale=x_scales[:, cols],
+                    lhsT=x_codes[:, n, cols].bitcast(FP8X4),
+                    lhsT_scale=x_scales[:, n, cols],
                     rhs=w_codes[:].bitcast(FP4X4),
                     rhs_scale=w_scales[:],
                     start=True,
                     stop=True,
                 )
-                nc.vector.tensor_tensor(out=out_sb[:, i, tau, :], in0=acc[:], in1=pos_b[:, tau, :], op=ADD)
-                if tl % 2 == 1:
-                    taus = slice(tau - 1, tau + 1)
-                    nc.sync.dma_start(out=out_view[i][:, taus, :], in_=out_sb[:, i, taus, :])
+                sums.append(acc)
+            return sums
+
+        def finish_step(n, sums):
+            pair, i = divmod(n, IMAGES)
+            for l in range(STEP_TILES):
+                tau = pair * STEP_TILES + l
+                nc.vector.tensor_tensor(out=out_sb[:, i, tau, :], in0=sums[l][:], in1=pos_b[:, tau, :], op=ADD)
+                nc.sync.dma_start(out=out_view[i][:, tau, :], in_=out_sb[:, i, tau, :])
 
         nc.vector.memset(w_scales[:].bitcast(I32), 0)
         nc.vector.memset(b_row[:], 0.0)
@@ -130,7 +123,7 @@ def tile_resampling_kernel(tc, encoded, W_words, W_scales, b, pos_emb, out):
         make_identity(nc, ident[:])
 
         nc.scalar.dma_start(out=b_row[0:1, :], in_=b.rearrange("(o f) -> o f", o=1))
-        load_group(0)
+        load_tokens(0, 0)
         nc.sync.dma_start(out=w_codes[:].bitcast(I32), in_=W_words[0].bitcast(I32))
         for quadrant in range(4):
             nc.sync.dma_start(
@@ -138,23 +131,31 @@ def tile_resampling_kernel(tc, encoded, W_words, W_scales, b, pos_emb, out):
                 in_=W_scales[0, 4 * quadrant : 4 * quadrant + 4, :].bitcast(I32),
             )
         load_pos(0)
-        load_group(1)
-        load_group(2)
+        load_tokens(1, 0)
         load_pos(1)
-        load_group(3)
+        load_tokens(0, 1)
+        load_pos(2)
+        load_tokens(1, 1)
+        load_pos(3)
 
         b_psum = acc_pool.tile([P, FEATURES], F32, tag="acc")
         nc.tensor.matmul(out=b_psum[:], lhsT=ones[:], rhs=b_row[:], start=True, stop=True)
-        nc.scalar.copy(out=b_all[:], in_=b_psum[:])
-        add_bias_to_pos(0)
-        add_bias_to_pos(1)
+        nc.vector.tensor_copy(out=b_all[:], in_=b_psum[:])
+        for tau in range(TOKENS_PER_PARTITION):
+            nc.gpsimd.tensor_tensor(out=pos_b[:, tau, :], in0=pos_sb[:, tau, :], in1=b_all[:], op=ADD)
 
-        sort_group(0)
-        banks = transpose_group(0)
-        for g in range(GROUPS):
-            if g + 1 < GROUPS:
-                sort_group(g + 1)
-            quantise_group(g, banks)
-            if g + 1 < GROUPS:
-                banks = transpose_group(g + 1)
-            project_group(g)
+        xts = {}
+        sort_step(0)
+        xts[0] = transpose_step(0)
+        sort_step(1)
+        quantise_step(0, xts[0])
+        xts[1] = transpose_step(1)
+        for n in range(STEPS):
+            if n + 2 < STEPS:
+                sort_step(n + 2)
+            if n + 1 < STEPS:
+                quantise_step(n + 1, xts[n + 1])
+            sums = multiply_step(n)
+            if n + 2 < STEPS:
+                xts[n + 2] = transpose_step(n + 2)
+            finish_step(n, sums)

@@ -33,8 +33,9 @@ def tile_resampling_kernel(tc, encoded, W_words, W_scales, b, pos_emb, out):
     nc = tc.nc
     with ExitStack() as ctx:
         keep = ctx.enter_context(tc.tile_pool(name="keep", bufs=1))
-        xt_pool = ctx.enter_context(tc.psum_pool(name="xt_pool", bufs=4))
+        xt_pool = ctx.enter_context(tc.psum_pool(name="xt_pool", bufs=3))
         acc_pool = ctx.enter_context(tc.psum_pool(name="acc_pool", bufs=4))
+        b_pool = ctx.enter_context(tc.psum_pool(name="b_pool", bufs=1))
         ctx.enter_context(tc.manual_schedule())
 
         x_sb = keep.tile([P, IMAGES, TAU_HALVES, 2, LOAD_TILES * K // 2], BF16)
@@ -50,7 +51,6 @@ def tile_resampling_kernel(tc, encoded, W_words, W_scales, b, pos_emb, out):
         ident = keep.tile([P, P], F32)
         ones = keep.tile([P, P], BF16)
         b_row = keep.tile([P, FEATURES], BF16)
-        b_all = keep.tile([P, FEATURES], F32)
 
         enc_view = encoded.rearrange(
             "i (y s a h e) d -> i s h y a (e d)", y=32, s=2, a=4, h=TAU_HALVES, e=2 * LOAD_TILES
@@ -65,6 +65,10 @@ def tile_resampling_kernel(tc, encoded, W_words, W_scales, b, pos_emb, out):
         def load_pos(pair):
             taus = slice(pair * STEP_TILES, (pair + 1) * STEP_TILES)
             nc.sync.dma_start(out=pos_sb[:, taus, :], in_=pos_view[:, taus, :])
+
+        def add_bias_to_pos(pair):
+            for tau in range(pair * STEP_TILES, (pair + 1) * STEP_TILES):
+                nc.vector.tensor_tensor(out=pos_b[:, tau, :], in0=b_psum[:], in1=pos_sb[:, tau, :], op=ADD)
 
         def sort_step(n):
             pair, i = divmod(n, IMAGES)
@@ -123,6 +127,7 @@ def tile_resampling_kernel(tc, encoded, W_words, W_scales, b, pos_emb, out):
         make_identity(nc, ident[:])
 
         nc.scalar.dma_start(out=b_row[0:1, :], in_=b.rearrange("(o f) -> o f", o=1))
+        load_pos(0)
         load_tokens(0, 0)
         nc.sync.dma_start(out=w_codes[:].bitcast(I32), in_=W_words[0].bitcast(I32))
         for quadrant in range(4):
@@ -130,19 +135,17 @@ def tile_resampling_kernel(tc, encoded, W_words, W_scales, b, pos_emb, out):
                 out=w_scales[32 * quadrant : 32 * quadrant + 4, :].bitcast(I32),
                 in_=W_scales[0, 4 * quadrant : 4 * quadrant + 4, :].bitcast(I32),
             )
-        load_pos(0)
-        load_tokens(1, 0)
         load_pos(1)
+        load_tokens(1, 0)
         load_tokens(0, 1)
         load_pos(2)
         load_tokens(1, 1)
         load_pos(3)
 
-        b_psum = acc_pool.tile([P, FEATURES], F32, tag="acc")
+        b_psum = b_pool.tile([P, FEATURES], F32)
         nc.tensor.matmul(out=b_psum[:], lhsT=ones[:], rhs=b_row[:], start=True, stop=True)
-        nc.vector.tensor_copy(out=b_all[:], in_=b_psum[:])
-        for tau in range(TOKENS_PER_PARTITION):
-            nc.gpsimd.tensor_tensor(out=pos_b[:, tau, :], in0=pos_sb[:, tau, :], in1=b_all[:], op=ADD)
+        add_bias_to_pos(0)
+        add_bias_to_pos(1)
 
         xts = {}
         sort_step(0)
@@ -159,3 +162,5 @@ def tile_resampling_kernel(tc, encoded, W_words, W_scales, b, pos_emb, out):
             if n + 2 < STEPS:
                 xts[n + 2] = transpose_step(n + 2)
             finish_step(n, sums)
+            if n % IMAGES == 0 and n // IMAGES + 2 < STEPS // IMAGES:
+                add_bias_to_pos(n // IMAGES + 2)

@@ -24,7 +24,6 @@ TILES = IMAGES * TOKENS_PER_PARTITION
 STEP_TILES = 2
 STEPS = TILES // STEP_TILES
 WORDS = K // 2
-HALF_WORDS = WORDS // 2
 
 FLOPS = 2 * IMAGES * TOKENS * K * FEATURES
 
@@ -33,13 +32,12 @@ def tile_resampling_kernel(tc, encoded, W_words, W_scales, b, pos_emb, out):
     nc = tc.nc
     with ExitStack() as ctx:
         keep = ctx.enter_context(tc.tile_pool(name="keep", bufs=1))
-        xt_pool = ctx.enter_context(tc.psum_pool(name="xt_pool", bufs=3))
+        xt_pool = ctx.enter_context(tc.psum_pool(name="xt_pool", bufs=4))
         acc_pool = ctx.enter_context(tc.psum_pool(name="acc_pool", bufs=4))
-        b_pool = ctx.enter_context(tc.psum_pool(name="b_pool", bufs=1))
         ctx.enter_context(tc.manual_schedule())
 
         x_sb = keep.tile([P, IMAGES, TAU_HALVES, 2, LOAD_TILES * K // 2], BF16)
-        sorted_words = keep.tile([P, STEPS, STEP_TILES, WORDS], F32)
+        sorted_words = keep.tile([P, STEPS, STEP_TILES, 2, P], F32)
         grouped = keep.tile([P, STEPS, STEP_TILES * P * 4], BF16, align_bytes=64)
         x_codes = keep.tile([P, STEPS, STEP_TILES * P], U32, align_bytes=64)
         x_scales = keep.tile([P, STEPS, STEP_TILES * P], U8, align_bytes=64)
@@ -51,6 +49,7 @@ def tile_resampling_kernel(tc, encoded, W_words, W_scales, b, pos_emb, out):
         ident = keep.tile([P, P], F32)
         ones = keep.tile([P, P], BF16)
         b_row = keep.tile([P, FEATURES], BF16)
+        b_all = keep.tile([P, FEATURES], F32)
 
         enc_view = encoded.rearrange(
             "i (y s a h e) d -> i s h y a (e d)", y=32, s=2, a=4, h=TAU_HALVES, e=2 * LOAD_TILES
@@ -66,28 +65,21 @@ def tile_resampling_kernel(tc, encoded, W_words, W_scales, b, pos_emb, out):
             taus = slice(pair * STEP_TILES, (pair + 1) * STEP_TILES)
             nc.sync.dma_start(out=pos_sb[:, taus, :], in_=pos_view[:, taus, :])
 
-        def add_bias_to_pos(pair):
-            for tau in range(pair * STEP_TILES, (pair + 1) * STEP_TILES):
-                nc.vector.tensor_tensor(out=pos_b[:, tau, :], in0=b_psum[:], in1=pos_sb[:, tau, :], op=ADD)
-
         def sort_step(n):
             pair, i = divmod(n, IMAGES)
-            for l in range(STEP_TILES):
-                h, tl = divmod(pair * STEP_TILES + l, LOAD_TILES)
-                for s in range(2):
-                    src = x_sb[:, i, h, s, tl * WORDS : (tl + 1) * WORDS].bitcast(F32)
-                    dst = sorted_words[:, n, l, s * HALF_WORDS : (s + 1) * HALF_WORDS]
-                    nc.scalar.copy(
-                        out=dst.rearrange("p (r c w) -> p r c w", r=8, c=2),
-                        in_=src.rearrange("p (c r w) -> p r c w", c=2, r=8),
-                    )
+            h, tl = divmod(pair * STEP_TILES, LOAD_TILES)
+            for s in range(2):
+                src = x_sb[:, i, h, s, tl * WORDS : (tl + STEP_TILES) * WORDS].bitcast(F32)
+                src = src.rearrange("p (l c r v u) -> p u l r c v", l=STEP_TILES, c=2, r=8, u=2)
+                for u in range(2):
+                    dst = sorted_words[:, n, :, u, s * (P // 2) : (s + 1) * (P // 2)]
+                    nc.scalar.copy(out=dst.rearrange("p l (r c v) -> p l r c v", r=8, c=2), in_=src[:, u])
 
         def transpose_step(n):
             xt = xt_pool.tile([P, STEP_TILES, 2, P], F32)
             for l in range(STEP_TILES):
-                planes = sorted_words[:, n, l, :].rearrange("p (j u) -> p u j", u=2)
                 for u in range(2):
-                    nc.tensor.transpose(xt[:, l, u, :], planes[:, u, :], ident[:])
+                    nc.tensor.transpose(xt[:, l, u, :], sorted_words[:, n, l, u, :], ident[:])
             return xt
 
         def quantise_step(n, xt):
@@ -127,7 +119,6 @@ def tile_resampling_kernel(tc, encoded, W_words, W_scales, b, pos_emb, out):
         make_identity(nc, ident[:])
 
         nc.scalar.dma_start(out=b_row[0:1, :], in_=b.rearrange("(o f) -> o f", o=1))
-        load_pos(0)
         load_tokens(0, 0)
         nc.sync.dma_start(out=w_codes[:].bitcast(I32), in_=W_words[0].bitcast(I32))
         for quadrant in range(4):
@@ -135,17 +126,19 @@ def tile_resampling_kernel(tc, encoded, W_words, W_scales, b, pos_emb, out):
                 out=w_scales[32 * quadrant : 32 * quadrant + 4, :].bitcast(I32),
                 in_=W_scales[0, 4 * quadrant : 4 * quadrant + 4, :].bitcast(I32),
             )
-        load_pos(1)
+        load_pos(0)
         load_tokens(1, 0)
+        load_pos(1)
         load_tokens(0, 1)
         load_pos(2)
         load_tokens(1, 1)
         load_pos(3)
 
-        b_psum = b_pool.tile([P, FEATURES], F32)
+        b_psum = acc_pool.tile([P, FEATURES], F32, tag="acc")
         nc.tensor.matmul(out=b_psum[:], lhsT=ones[:], rhs=b_row[:], start=True, stop=True)
-        add_bias_to_pos(0)
-        add_bias_to_pos(1)
+        nc.vector.tensor_copy(out=b_all[:], in_=b_psum[:])
+        for tau in range(TOKENS_PER_PARTITION):
+            nc.gpsimd.tensor_tensor(out=pos_b[:, tau, :], in0=pos_sb[:, tau, :], in1=b_all[:], op=ADD)
 
         xts = {}
         sort_step(0)
@@ -162,5 +155,3 @@ def tile_resampling_kernel(tc, encoded, W_words, W_scales, b, pos_emb, out):
             if n + 2 < STEPS:
                 xts[n + 2] = transpose_step(n + 2)
             finish_step(n, sums)
-            if n % IMAGES == 0 and n // IMAGES + 2 < STEPS // IMAGES:
-                add_bias_to_pos(n // IMAGES + 2)

@@ -61,6 +61,12 @@ def tile_resampling_kernel(tc, encoded, W_words, W_scales, b, pos_emb, out):
             for s in range(2):
                 nc.sync.dma_start(out=x_sb[:, i, h, s, :], in_=enc_view[i, s, h])
 
+        def load_step_tokens(i, pair):
+            h, tl = divmod(pair * STEP_TILES, LOAD_TILES)
+            cols = slice(tl * K // 2, (tl + STEP_TILES) * K // 2)
+            for s in range(2):
+                nc.sync.dma_start(out=x_sb[:, i, h, s, cols], in_=enc_view[i, s, h][:, :, cols])
+
         def load_pos(pair):
             taus = slice(pair * STEP_TILES, (pair + 1) * STEP_TILES)
             nc.sync.dma_start(out=pos_sb[:, taus, :], in_=pos_view[:, taus, :])
@@ -113,21 +119,23 @@ def tile_resampling_kernel(tc, encoded, W_words, W_scales, b, pos_emb, out):
                 nc.vector.tensor_tensor(out=out_sb[:, i, tau, :], in0=sums[l][:], in1=pos_b[:, tau, :], op=ADD)
                 nc.sync.dma_start(out=out_view[i][:, tau, :], in_=out_sb[:, i, tau, :])
 
-        nc.vector.memset(w_scales[:].bitcast(I32), 0)
         nc.vector.memset(b_row[:], 0.0)
+        nc.vector.memset(w_scales[:].bitcast(I32), 0)
         nc.vector.memset(ones[:], 1.0)
         make_identity(nc, ident[:])
 
-        nc.scalar.dma_start(out=b_row[0:1, :], in_=b.rearrange("(o f) -> o f", o=1))
-        load_tokens(0, 0)
+        load_step_tokens(0, 0)
+        nc.sync.dma_start(out=b_row[0:1, :], in_=b.rearrange("(o f) -> o f", o=1))
+        load_step_tokens(1, 0)
+        load_pos(0)
+        load_step_tokens(0, 1)
         nc.sync.dma_start(out=w_codes[:].bitcast(I32), in_=W_words[0].bitcast(I32))
         for quadrant in range(4):
             nc.sync.dma_start(
                 out=w_scales[32 * quadrant : 32 * quadrant + 4, :].bitcast(I32),
                 in_=W_scales[0, 4 * quadrant : 4 * quadrant + 4, :].bitcast(I32),
             )
-        load_pos(0)
-        load_tokens(1, 0)
+        load_step_tokens(1, 1)
         load_pos(1)
         load_tokens(0, 1)
         load_pos(2)
@@ -141,17 +149,14 @@ def tile_resampling_kernel(tc, encoded, W_words, W_scales, b, pos_emb, out):
             nc.gpsimd.tensor_tensor(out=pos_b[:, tau, :], in0=pos_sb[:, tau, :], in1=b_all[:], op=ADD)
 
         xts = {}
-        sort_step(0)
-        xts[0] = transpose_step(0)
-        sort_step(1)
-        quantise_step(0, xts[0])
-        xts[1] = transpose_step(1)
-        for n in range(STEPS):
-            if n + 2 < STEPS:
-                sort_step(n + 2)
-            if n + 1 < STEPS:
-                quantise_step(n + 1, xts[n + 1])
-            sums = multiply_step(n)
-            if n + 2 < STEPS:
-                xts[n + 2] = transpose_step(n + 2)
-            finish_step(n, sums)
+        for t in range(-3, STEPS):
+            if 0 <= t + 1 < STEPS:
+                quantise_step(t + 1, xts[t + 1])
+            if t + 3 < STEPS:
+                sort_step(t + 3)
+            if t >= 0:
+                sums = multiply_step(t)
+            if 0 <= t + 2 < STEPS:
+                xts[t + 2] = transpose_step(t + 2)
+            if t >= 0:
+                finish_step(t, sums)

@@ -24,6 +24,7 @@ TILES = IMAGES * TOKENS_PER_PARTITION
 STEP_TILES = 2
 STEPS = TILES // STEP_TILES
 WORDS = K // 2
+FIRST_GPSIMD_TAU = 2
 
 FLOPS = 2 * IMAGES * TOKENS * K * FEATURES
 
@@ -116,7 +117,7 @@ def tile_resampling_kernel(tc, encoded, W_words, W_scales, b, pos_emb, out):
             pair, i = divmod(n, IMAGES)
             for l in range(STEP_TILES):
                 tau = pair * STEP_TILES + l
-                nc.vector.tensor_tensor(out=out_sb[:, i, tau, :], in0=sums[l][:], in1=pos_b[:, tau, :], op=ADD)
+                nc.vector.tensor_tensor(out=out_sb[:, i, tau, :], in0=sums[l][:], in1=pos_b_of[tau], op=ADD)
                 nc.sync.dma_start(out=out_view[i][:, tau, :], in_=out_sb[:, i, tau, :])
 
         nc.vector.memset(b_row[:], 0.0)
@@ -145,13 +146,20 @@ def tile_resampling_kernel(tc, encoded, W_words, W_scales, b, pos_emb, out):
         b_psum = acc_pool.tile([P, FEATURES], F32, tag="acc")
         nc.tensor.matmul(out=b_psum[:], lhsT=ones[:], rhs=b_row[:], start=True, stop=True)
         nc.vector.tensor_copy(out=b_all[:], in_=b_psum[:])
+        pos_b_of = {}
         for tau in range(TOKENS_PER_PARTITION):
-            nc.gpsimd.tensor_tensor(out=pos_b[:, tau, :], in0=pos_sb[:, tau, :], in1=b_all[:], op=ADD)
+            pos_b_of[tau] = pos_b[:, tau, :]
+        pos_b_of[FIRST_GPSIMD_TAU] = grouped[:, 1, :].bitcast(F32)
+        for tau in range(FIRST_GPSIMD_TAU):
+            nc.vector.tensor_tensor(out=pos_b_of[tau], in0=b_psum[:], in1=pos_sb[:, tau, :], op=ADD)
 
         xts = {}
         for t in range(-3, STEPS):
             if 0 <= t + 1 < STEPS:
                 quantise_step(t + 1, xts[t + 1])
+            if t == 0:
+                for tau in range(FIRST_GPSIMD_TAU, TOKENS_PER_PARTITION):
+                    nc.gpsimd.tensor_tensor(out=pos_b_of[tau], in0=pos_sb[:, tau, :], in1=b_all[:], op=ADD)
             if t + 3 < STEPS:
                 sort_step(t + 3)
             if t >= 0:

@@ -51,6 +51,7 @@ def tile_resampling_kernel(tc, encoded, W_words, W_scales, b, pos_emb, out):
         ones = keep.tile([P, P], BF16)
         b_row = keep.tile([P, FEATURES], BF16)
         b_all = keep.tile([P, FEATURES], F32)
+        zeros = keep.tile([P, FEATURES], BF16)
 
         enc_view = encoded.rearrange(
             "i (y s a h e) d -> i s h y a (e d)", y=32, s=2, a=4, h=TAU_HALVES, e=2 * LOAD_TILES
@@ -113,6 +114,10 @@ def tile_resampling_kernel(tc, encoded, W_words, W_scales, b, pos_emb, out):
                 sums.append(acc)
             return sums
 
+        def warm_up():
+            idle = acc_pool.tile([P, FEATURES], F32, tag="acc")
+            nc.tensor.matmul(out=idle[:], lhsT=ones[:], rhs=zeros[:], start=True, stop=True)
+
         def finish_step(n, sums):
             pair, i = divmod(n, IMAGES)
             for l in range(STEP_TILES):
@@ -121,6 +126,7 @@ def tile_resampling_kernel(tc, encoded, W_words, W_scales, b, pos_emb, out):
                 nc.sync.dma_start(out=out_view[i][:, tau, :], in_=out_sb[:, i, tau, :])
 
         nc.vector.memset(b_row[:], 0.0)
+        nc.gpsimd.memset(zeros[:], 0.0)
         nc.vector.memset(w_scales[:].bitcast(I32), 0)
         nc.vector.memset(ones[:], 1.0)
         make_identity(nc, ident[:])
@@ -143,6 +149,8 @@ def tile_resampling_kernel(tc, encoded, W_words, W_scales, b, pos_emb, out):
         load_tokens(1, 1)
         load_pos(3)
 
+        warm_up()
+        warm_up()
         b_psum = acc_pool.tile([P, FEATURES], F32, tag="acc")
         nc.tensor.matmul(out=b_psum[:], lhsT=ones[:], rhs=b_row[:], start=True, stop=True)
         nc.vector.tensor_copy(out=b_all[:], in_=b_psum[:])
@@ -166,5 +174,7 @@ def tile_resampling_kernel(tc, encoded, W_words, W_scales, b, pos_emb, out):
                 sums = multiply_step(t)
             if 0 <= t + 2 < STEPS:
                 xts[t + 2] = transpose_step(t + 2)
+            if t < 0:
+                warm_up()
             if t >= 0:
                 finish_step(t, sums)

@@ -24,6 +24,7 @@ TILES = IMAGES * TOKENS_PER_PARTITION
 STEP_TILES = 2
 STEPS = TILES // STEP_TILES
 WORDS = K // 2
+EARLY_WARM_UPS = 4
 FIRST_GPSIMD_TAU = 2
 
 FLOPS = 2 * IMAGES * TOKENS * K * FEATURES
@@ -48,10 +49,10 @@ def tile_resampling_kernel(tc, encoded, W_words, W_scales, b, pos_emb, out):
         pos_b = keep.tile([P, TOKENS_PER_PARTITION, FEATURES], F32)
         out_sb = keep.tile([P, IMAGES, TOKENS_PER_PARTITION, FEATURES], F32)
         ident = keep.tile([P, P], F32)
+        nothing = keep.tile([P, P], F32)
         ones = keep.tile([P, P], BF16)
         b_row = keep.tile([P, FEATURES], BF16)
         b_all = keep.tile([P, FEATURES], F32)
-        zeros = keep.tile([P, FEATURES], BF16)
 
         enc_view = encoded.rearrange(
             "i (y s a h e) d -> i s h y a (e d)", y=32, s=2, a=4, h=TAU_HALVES, e=2 * LOAD_TILES
@@ -116,7 +117,7 @@ def tile_resampling_kernel(tc, encoded, W_words, W_scales, b, pos_emb, out):
 
         def warm_up():
             idle = acc_pool.tile([P, FEATURES], F32, tag="acc")
-            nc.tensor.matmul(out=idle[:], lhsT=ones[:], rhs=zeros[:], start=True, stop=True)
+            nc.tensor.matmul(out=idle[:, 0:P], lhsT=nothing[:], rhs=nothing[:], start=True, stop=True)
 
         def finish_step(n, sums):
             pair, i = divmod(n, IMAGES)
@@ -125,8 +126,8 @@ def tile_resampling_kernel(tc, encoded, W_words, W_scales, b, pos_emb, out):
                 nc.vector.tensor_tensor(out=out_sb[:, i, tau, :], in0=sums[l][:], in1=pos_b_of[tau], op=ADD)
                 nc.sync.dma_start(out=out_view[i][:, tau, :], in_=out_sb[:, i, tau, :])
 
+        nc.gpsimd.memset(nothing[:], 0.0)
         nc.vector.memset(b_row[:], 0.0)
-        nc.gpsimd.memset(zeros[:], 0.0)
         nc.vector.memset(w_scales[:].bitcast(I32), 0)
         nc.vector.memset(ones[:], 1.0)
         make_identity(nc, ident[:])
@@ -145,12 +146,12 @@ def tile_resampling_kernel(tc, encoded, W_words, W_scales, b, pos_emb, out):
         load_step_tokens(1, 1)
         load_pos(1)
         load_tokens(0, 1)
-        load_pos(2)
         load_tokens(1, 1)
+        load_pos(2)
         load_pos(3)
 
-        warm_up()
-        warm_up()
+        for early in range(EARLY_WARM_UPS):
+            warm_up()
         b_psum = acc_pool.tile([P, FEATURES], F32, tag="acc")
         nc.tensor.matmul(out=b_psum[:], lhsT=ones[:], rhs=b_row[:], start=True, stop=True)
         nc.vector.tensor_copy(out=b_all[:], in_=b_psum[:])

@@ -124,7 +124,11 @@ def tile_resampling_kernel(tc, encoded, W_words, W_scales, b, pos_emb, out):
             for l in range(STEP_TILES):
                 tau = pair * STEP_TILES + l
                 nc.vector.tensor_tensor(out=out_sb[:, i, tau, :], in0=sums[l][:], in1=pos_b_of[tau], op=ADD)
-                nc.sync.dma_start(out=out_view[i][:, tau, :], in_=out_sb[:, i, tau, :])
+                if n == STEPS - 1:
+                    nc.sync.dma_start(out=out_view[i][:, tau, :], in_=out_sb[:, i, tau, :])
+            if n < STEPS - 1:
+                taus = slice(pair * STEP_TILES, (pair + 1) * STEP_TILES)
+                nc.sync.dma_start(out=out_view[i][:, taus, :], in_=out_sb[:, i, taus, :])
 
         nc.gpsimd.memset(nothing[:], 0.0)
         nc.vector.memset(b_row[:], 0.0)

@@ -84,19 +84,32 @@ def tile_resampling_kernel(tc, encoded, W_words, W_scales, b, pos_emb, out):
                     dst = sorted_words[:, n, :, u, s * (P // 2) : (s + 1) * (P // 2)]
                     nc.scalar.copy(out=dst.rearrange("p l (r c v) -> p l r c v", r=8, c=2), in_=src[:, u])
 
-        def transpose_step(n):
-            xt = xt_pool.tile([P, STEP_TILES, 2, P], F32)
-            for l in range(STEP_TILES):
-                for u in range(2):
-                    nc.tensor.transpose(xt[:, l, u, :], sorted_words[:, n, l, u, :], ident[:])
-            return xt
+        def portions(n):
+            if n == 0:
+                return [(0, 1), (1, 1)]
+            return [(0, STEP_TILES)]
 
-        def quantise_step(n, xt):
-            nc.scalar.copy(
-                out=grouped[:, n, :].bitcast(F32).rearrange("p (l m u) -> p l m u", l=STEP_TILES, u=2),
-                in_=xt[:].rearrange("p l u m -> p l m u"),
-            )
-            nc.vector.quantize_mx(out=x_codes[:, n, :].bitcast(FP8X4), scales=x_scales[:, n, :], in_=grouped[:, n, :])
+        def transpose_step(n):
+            banks = []
+            for first, count in portions(n):
+                xt = xt_pool.tile([P, count, 2, P], F32)
+                for l in range(count):
+                    for u in range(2):
+                        nc.tensor.transpose(xt[:, l, u, :], sorted_words[:, n, first + l, u, :], ident[:])
+                banks.append(xt)
+            return banks
+
+        def quantise_step(n, banks):
+            for (first, count), xt in zip(portions(n), banks):
+                tokens = slice(first * P, (first + count) * P)
+                values = slice(first * P * 4, (first + count) * P * 4)
+                nc.scalar.copy(
+                    out=grouped[:, n, values].bitcast(F32).rearrange("p (l m u) -> p l m u", l=count, u=2),
+                    in_=xt[:].rearrange("p l u m -> p l m u"),
+                )
+                nc.vector.quantize_mx(
+                    out=x_codes[:, n, tokens].bitcast(FP8X4), scales=x_scales[:, n, tokens], in_=grouped[:, n, values]
+                )
 
         def multiply_step(n):
             sums = []

@@ -24,7 +24,7 @@ TILES = IMAGES * TOKENS_PER_PARTITION
 STEP_TILES = 2
 STEPS = TILES // STEP_TILES
 WORDS = K // 2
-EARLY_WARM_UPS = 4
+EARLY_WARM_UPS = 2
 FIRST_GPSIMD_TAU = 2
 
 FLOPS = 2 * IMAGES * TOKENS * K * FEATURES
@@ -79,10 +79,9 @@ def tile_resampling_kernel(tc, encoded, W_words, W_scales, b, pos_emb, out):
             h, tl = divmod(pair * STEP_TILES, LOAD_TILES)
             for s in range(2):
                 src = x_sb[:, i, h, s, tl * WORDS : (tl + STEP_TILES) * WORDS].bitcast(F32)
-                src = src.rearrange("p (l c r v u) -> p u l r c v", l=STEP_TILES, c=2, r=8, u=2)
-                for u in range(2):
-                    dst = sorted_words[:, n, :, u, s * (P // 2) : (s + 1) * (P // 2)]
-                    nc.scalar.copy(out=dst.rearrange("p l (r c v) -> p l r c v", r=8, c=2), in_=src[:, u])
+                src = src.rearrange("p (l c r v u) -> p l u c r v", l=STEP_TILES, c=2, r=8, u=2)
+                dst = sorted_words[:, n, :, :, s * (P // 2) : (s + 1) * (P // 2)]
+                nc.scalar.copy(out=dst.rearrange("p l u (r c v) -> p l u c r v", r=8, c=2), in_=src)
 
         def portions(n):
             if n == 0:
@@ -143,8 +142,8 @@ def tile_resampling_kernel(tc, encoded, W_words, W_scales, b, pos_emb, out):
                 taus = slice(pair * STEP_TILES, (pair + 1) * STEP_TILES)
                 nc.sync.dma_start(out=out_view[i][:, taus, :], in_=out_sb[:, i, taus, :])
 
+        nc.gpsimd.memset(b_row[:].bitcast(F32), 0.0)
         nc.gpsimd.memset(nothing[:], 0.0)
-        nc.vector.memset(b_row[:], 0.0)
         nc.vector.memset(w_scales[:].bitcast(I32), 0)
         nc.vector.memset(ones[:], 1.0)
         make_identity(nc, ident[:])
@@ -192,7 +191,7 @@ def tile_resampling_kernel(tc, encoded, W_words, W_scales, b, pos_emb, out):
                 sums = multiply_step(t)
             if 0 <= t + 2 < STEPS:
                 xts[t + 2] = transpose_step(t + 2)
-            if t < 0:
+            if -3 < t < 0:
                 warm_up()
             if t >= 0:
                 finish_step(t, sums)

@@ -25,6 +25,7 @@ STEP_TILES = 2
 STEPS = TILES // STEP_TILES
 WORDS = K // 2
 EARLY_WARM_UPS = 2
+SINGLE_STORES_FROM = 6
 FIRST_GPSIMD_TAU = 2
 
 FLOPS = 2 * IMAGES * TOKENS * K * FEATURES
@@ -136,9 +137,9 @@ def tile_resampling_kernel(tc, encoded, W_words, W_scales, b, pos_emb, out):
             for l in range(STEP_TILES):
                 tau = pair * STEP_TILES + l
                 nc.vector.tensor_tensor(out=out_sb[:, i, tau, :], in0=sums[l][:], in1=pos_b_of[tau], op=ADD)
-                if n == STEPS - 1:
+                if n >= SINGLE_STORES_FROM:
                     nc.sync.dma_start(out=out_view[i][:, tau, :], in_=out_sb[:, i, tau, :])
-            if n < STEPS - 1:
+            if n < SINGLE_STORES_FROM:
                 taus = slice(pair * STEP_TILES, (pair + 1) * STEP_TILES)
                 nc.sync.dma_start(out=out_view[i][:, taus, :], in_=out_sb[:, i, taus, :])
 

@@ -148,6 +148,9 @@ def tile_resampling_kernel(tc, encoded, W_words, W_scales, b, pos_emb, out):
         nc.vector.memset(w_scales[:].bitcast(I32), 0)
         nc.vector.memset(ones[:], 1.0)
         make_identity(nc, ident[:])
+        nc.gpsimd.dma_start(
+            out=pos_sb[:, STEP_TILES : 2 * STEP_TILES, :], in_=pos_emb.rearrange("(p t) f -> p t f", t=TOKENS_PER_PARTITION)[:, STEP_TILES : 2 * STEP_TILES, :]
+        )
 
         load_step_tokens(0, 0)
         nc.sync.dma_start(out=b_row[0:1, :], in_=b.rearrange("(o f) -> o f", o=1))
@@ -161,7 +164,6 @@ def tile_resampling_kernel(tc, encoded, W_words, W_scales, b, pos_emb, out):
                 in_=W_scales[0, 4 * quadrant : 4 * quadrant + 4, :].bitcast(I32),
             )
         load_step_tokens(1, 1)
-        load_pos(1)
         load_tokens(0, 1)
         load_tokens(1, 1)
         load_pos(2)

from contextlib import ExitStack

import concourse.mybir as mybir
from concourse.masks import make_identity

F32 = mybir.dt.float32
BF16 = mybir.dt.bfloat16
I32 = mybir.dt.int32
U32 = mybir.dt.uint32
U8 = mybir.dt.uint8
FP8X4 = mybir.dt.float8_e4m3fn_x4
FP4X4 = mybir.dt.float4_e2m1fn_x4
ADD = mybir.AluOpType.add

P = 128
IMAGES = 2
TOKENS = 1024
K = 512
FEATURES = 512
TOKENS_PER_PARTITION = TOKENS // P
LOAD_TILES = 4
TAU_HALVES = TOKENS_PER_PARTITION // LOAD_TILES
TILES = IMAGES * TOKENS_PER_PARTITION
STEP_TILES = 2
STEPS = TILES // STEP_TILES
WORDS = K // 2
EARLY_WARM_UPS = 2
SINGLE_STORES_FROM = 6
FIRST_GPSIMD_TAU = 2

FLOPS = 2 * IMAGES * TOKENS * K * FEATURES


def tile_resampling_kernel(tc, encoded, W_words, W_scales, b, pos_emb, out):
    nc = tc.nc
    with ExitStack() as ctx:
        keep = ctx.enter_context(tc.tile_pool(name="keep", bufs=1))
        xt_pool = ctx.enter_context(tc.psum_pool(name="xt_pool", bufs=4))
        acc_pool = ctx.enter_context(tc.psum_pool(name="acc_pool", bufs=4))
        ctx.enter_context(tc.manual_schedule())

        x_sb = keep.tile([P, IMAGES, TAU_HALVES, 2, LOAD_TILES * K // 2], BF16)
        sorted_words = keep.tile([P, STEPS, STEP_TILES, 2, P], F32)
        grouped = keep.tile([P, STEPS, STEP_TILES * P * 4], BF16, align_bytes=64)
        x_codes = keep.tile([P, STEPS, STEP_TILES * P], U32, align_bytes=64)
        x_scales = keep.tile([P, STEPS, STEP_TILES * P], U8, align_bytes=64)
        w_codes = keep.tile([P, 2 * FEATURES], U8, align_bytes=64)
        w_scales = keep.tile([P, FEATURES], U8, align_bytes=64)
        pos_sb = keep.tile([P, TOKENS_PER_PARTITION, FEATURES], BF16)
        pos_b = keep.tile([P, TOKENS_PER_PARTITION, FEATURES], F32)
        out_sb = keep.tile([P, IMAGES, TOKENS_PER_PARTITION, FEATURES], F32)
        ident = keep.tile([P, P], F32)
        nothing = keep.tile([P, P], F32)
        ones = keep.tile([P, P], BF16)
        b_row = keep.tile([P, FEATURES], BF16)
        b_all = keep.tile([P, FEATURES], F32)

        enc_view = encoded.rearrange(
            "i (y s a h e) d -> i s h y a (e d)", y=32, s=2, a=4, h=TAU_HALVES, e=2 * LOAD_TILES
        )
        pos_view = pos_emb.rearrange("(p t) f -> p t f", t=TOKENS_PER_PARTITION)
        out_view = out.rearrange("i (p t) f -> i p t f", t=TOKENS_PER_PARTITION)

        def load_tokens(i, h):
            for s in range(2):
                nc.sync.dma_start(out=x_sb[:, i, h, s, :], in_=enc_view[i, s, h])

        def load_step_tokens(i, pair):
            h, tl = divmod(pair * STEP_TILES, LOAD_TILES)
            cols = slice(tl * K // 2, (tl + STEP_TILES) * K // 2)
            for s in range(2):
                nc.sync.dma_start(out=x_sb[:, i, h, s, cols], in_=enc_view[i, s, h][:, :, cols])

        def load_pos(pair):
            taus = slice(pair * STEP_TILES, (pair + 1) * STEP_TILES)
            nc.sync.dma_start(out=pos_sb[:, taus, :], in_=pos_view[:, taus, :])

        def sort_step(n):
            pair, i = divmod(n, IMAGES)
            h, tl = divmod(pair * STEP_TILES, LOAD_TILES)
            for s in range(2):
                src = x_sb[:, i, h, s, tl * WORDS : (tl + STEP_TILES) * WORDS].bitcast(F32)
                src = src.rearrange("p (l c r v u) -> p l u c r v", l=STEP_TILES, c=2, r=8, u=2)
                dst = sorted_words[:, n, :, :, s * (P // 2) : (s + 1) * (P // 2)]
                nc.scalar.copy(out=dst.rearrange("p l u (r c v) -> p l u c r v", r=8, c=2), in_=src)

        def portions(n):
            if n == 0:
                return [(0, 1), (1, 1)]
            return [(0, STEP_TILES)]

        def transpose_step(n):
            banks = []
            for first, count in portions(n):
                xt = xt_pool.tile([P, count, 2, P], F32)
                for l in range(count):
                    for u in range(2):
                        nc.tensor.transpose(xt[:, l, u, :], sorted_words[:, n, first + l, u, :], ident[:])
                banks.append(xt)
            return banks

        def quantise_step(n, banks):
            for (first, count), xt in zip(portions(n), banks):
                tokens = slice(first * P, (first + count) * P)
                values = slice(first * P * 4, (first + count) * P * 4)
                nc.scalar.copy(
                    out=grouped[:, n, values].bitcast(F32).rearrange("p (l m u) -> p l m u", l=count, u=2),
                    in_=xt[:].rearrange("p l u m -> p l m u"),
                )
                nc.vector.quantize_mx(
                    out=x_codes[:, n, tokens].bitcast(FP8X4), scales=x_scales[:, n, tokens], in_=grouped[:, n, values]
                )

        def multiply_step(n):
            sums = []
            for l in range(STEP_TILES):
                cols = slice(l * P, (l + 1) * P)
                acc = acc_pool.tile([P, FEATURES], F32, tag="acc")
                nc.tensor.matmul_mx(
                    out=acc[:],
                    lhsT=x_codes[:, n, cols].bitcast(FP8X4),
                    lhsT_scale=x_scales[:, n, cols],
                    rhs=w_codes[:].bitcast(FP4X4),
                    rhs_scale=w_scales[:],
                    start=True,
                    stop=True,
                )
                sums.append(acc)
            return sums

        def warm_up():
            idle = acc_pool.tile([P, FEATURES], F32, tag="acc")
            nc.tensor.matmul(out=idle[:, 0:P], lhsT=nothing[:], rhs=nothing[:], start=True, stop=True)

        def finish_step(n, sums):
            pair, i = divmod(n, IMAGES)
            for l in range(STEP_TILES):
                tau = pair * STEP_TILES + l
                nc.vector.tensor_tensor(out=out_sb[:, i, tau, :], in0=sums[l][:], in1=pos_b_of[tau], op=ADD)
                if n >= SINGLE_STORES_FROM:
                    nc.sync.dma_start(out=out_view[i][:, tau, :], in_=out_sb[:, i, tau, :])
            if n < SINGLE_STORES_FROM:
                taus = slice(pair * STEP_TILES, (pair + 1) * STEP_TILES)
                nc.sync.dma_start(out=out_view[i][:, taus, :], in_=out_sb[:, i, taus, :])

        nc.gpsimd.memset(b_row[:].bitcast(F32), 0.0)
        nc.gpsimd.memset(nothing[:], 0.0)
        nc.vector.memset(w_scales[:].bitcast(I32), 0)
        nc.vector.memset(ones[:], 1.0)
        make_identity(nc, ident[:])
        nc.gpsimd.dma_start(
            out=pos_sb[:, STEP_TILES : 2 * STEP_TILES, :], in_=pos_emb.rearrange("(p t) f -> p t f", t=TOKENS_PER_PARTITION)[:, STEP_TILES : 2 * STEP_TILES, :]
        )

        load_step_tokens(0, 0)
        nc.sync.dma_start(out=b_row[0:1, :], in_=b.rearrange("(o f) -> o f", o=1))
        load_step_tokens(1, 0)
        load_pos(0)
        load_step_tokens(0, 1)
        nc.sync.dma_start(out=w_codes[:].bitcast(I32), in_=W_words[0].bitcast(I32))
        for quadrant in range(4):
            nc.sync.dma_start(
                out=w_scales[32 * quadrant : 32 * quadrant + 4, :].bitcast(I32),
                in_=W_scales[0, 4 * quadrant : 4 * quadrant + 4, :].bitcast(I32),
            )
        load_step_tokens(1, 1)
        load_tokens(0, 1)
        load_tokens(1, 1)
        load_pos(2)
        load_pos(3)

        for early in range(EARLY_WARM_UPS):
            warm_up()
        b_psum = acc_pool.tile([P, FEATURES], F32, tag="acc")
        nc.tensor.matmul(out=b_psum[:], lhsT=ones[:], rhs=b_row[:], start=True, stop=True)
        nc.vector.tensor_copy(out=b_all[:], in_=b_psum[:])
        pos_b_of = {}
        for tau in range(TOKENS_PER_PARTITION):
            pos_b_of[tau] = pos_b[:, tau, :]
        pos_b_of[FIRST_GPSIMD_TAU] = grouped[:, 1, :].bitcast(F32)
        for tau in range(FIRST_GPSIMD_TAU):
            nc.vector.tensor_tensor(out=pos_b_of[tau], in0=b_psum[:], in1=pos_sb[:, tau, :], op=ADD)

        xts = {}
        for t in range(-3, STEPS):
            if 0 <= t + 1 < STEPS:
                quantise_step(t + 1, xts[t + 1])
            if t == 0:
                for tau in range(FIRST_GPSIMD_TAU, TOKENS_PER_PARTITION):
                    nc.gpsimd.tensor_tensor(out=pos_b_of[tau], in0=pos_sb[:, tau, :], in1=b_all[:], op=ADD)
            if t + 3 < STEPS:
                sort_step(t + 3)
            if t >= 0:
                sums = multiply_step(t)
            if 0 <= t + 2 < STEPS:
                xts[t + 2] = transpose_step(t + 2)
            if -3 < t < 0:
                warm_up()
            if t >= 0:
                finish_step(t, sums)
